import numpy as np
import ml_dtypes

BF16 = ml_dtypes.bfloat16


def bf(x):
    return np.asarray(x, np.float32).astype(BF16)


def f32(x):
    return np.asarray(x, np.float32)


def f64(x):
    return np.asarray(x).astype(np.float64)


def striped(idx):
    return np.tile(idx.reshape(-1, 16).T, (8, 1))


C, S, K, H, N = 256, 512, 4, 256, 1024
SCALE = np.sqrt(C)


def setup_inputs():
    idx = np.concatenate([np.random.permutation(S)[:H] for _ in range(K)])
    return {"emb": f32(0.1 * np.random.standard_normal((C, S))), "pos": f32(0.5 * np.random.standard_normal((C, H))), "offs": striped(idx)}


def reference(emb, pos, offs):
    idx = offs[:16].T.reshape(-1)
    return SCALE * f64(emb)[:, idx] + np.tile(f64(pos), (1, K))

@@ -1,0 +1,39 @@
+import concourse.mybir as mybir
+
+F32 = mybir.dt.float32
+U16 = mybir.dt.uint16
+ADD = mybir.AluOpType.add
+
+P = 128
+C, S, K, H = 256, 512, 4, 256
+N = K * H
+SCALE = 16.0
+BLOCKS = C // P
+LIST_COLUMNS = H // 16
+
+
+def tile_musictransformercontinuoustoken_kernel(tc, emb, pos, offs, out):
+    nc = tc.nc
+    with tc.tile_pool(name="held", bufs=1) as held:
+        offsets = held.tile([P, N // 16], U16, name="offsets")
+        nc.sync.dma_start(offsets[:], offs)
+
+        raw, place = [], []
+        for b in range(BLOCKS):
+            rows = slice(b * P, (b + 1) * P)
+            raw.append(held.tile([P, S], F32, name=f"raw{b}"))
+            place.append(held.tile([P, H], F32, name=f"place{b}"))
+            nc.sync.dma_start(raw[b][:], emb[rows, :])
+            nc.scalar.dma_start(place[b][:], pos[rows, :])
+
+        for b in range(BLOCKS):
+            rows = slice(b * P, (b + 1) * P)
+            table = held.tile([P, S], F32, name=f"table{b}")
+            nc.scalar.mul(table[:], raw[b][:], SCALE)
+
+            result = held.tile([P, N], F32, name=f"result{b}")
+            for k in range(K):
+                columns = slice(k * H, (k + 1) * H)
+                tokens = offsets[:, k * LIST_COLUMNS : (k + 1) * LIST_COLUMNS]
+                nc.vector.tensor_tensor(result[:, columns], table[:].indirect(tokens), place[b][:], ADD)
+                nc.sync.dma_start(out[rows, columns], result[:, columns])

@@ -23,17 +23,18 @@ def tile_musictransformercontinuoustoken_kernel(tc, emb, pos, offs, out):
             rows = slice(b * P, (b + 1) * P)
             raw.append(held.tile([P, S], F32, name=f"raw{b}"))
             place.append(held.tile([P, H], F32, name=f"place{b}"))
-            nc.sync.dma_start(raw[b][:], emb[rows, :])
-            nc.scalar.dma_start(place[b][:], pos[rows, :])
+            nc.scalar.dma_start(raw[b][:], emb[rows, :])
+            nc.sync.dma_start(place[b][:], pos[rows, :])
+
+        table = [held.tile([P, S], F32, name=f"table{b}") for b in range(BLOCKS)]
+        nc.vector.tensor_scalar_mul(table[0][:], raw[0][:], SCALE)
+        nc.scalar.mul(table[1][:], raw[1][:], SCALE)
 
         for b in range(BLOCKS):
             rows = slice(b * P, (b + 1) * P)
-            table = held.tile([P, S], F32, name=f"table{b}")
-            nc.scalar.mul(table[:], raw[b][:], SCALE)
-
             result = held.tile([P, N], F32, name=f"result{b}")
             for k in range(K):
                 columns = slice(k * H, (k + 1) * H)
                 tokens = offsets[:, k * LIST_COLUMNS : (k + 1) * LIST_COLUMNS]
-                nc.vector.tensor_tensor(result[:, columns], table[:].indirect(tokens), place[b][:], ADD)
+                nc.vector.tensor_tensor(result[:, columns], table[b][:].indirect(tokens), place[b][:], ADD)
                 nc.sync.dma_start(out[rows, columns], result[:, columns])

@@ -16,19 +16,21 @@ def tile_musictransformercontinuoustoken_kernel(tc, emb, pos, offs, out):
     nc = tc.nc
     with tc.tile_pool(name="held", bufs=1) as held:
         offsets = held.tile([P, N // 16], U16, name="offsets")
+        raw = [held.tile([P, S], F32, name=f"raw{b}") for b in range(BLOCKS)]
+        place = [held.tile([P, H], F32, name=f"place{b}") for b in range(BLOCKS)]
+
+        nc.scalar.dma_start(raw[0][:], emb[0:P, :])
+        nc.sync.dma_start(place[0][:], pos[0:P, :])
         nc.sync.dma_start(offsets[:], offs)
+        nc.scalar.dma_start(raw[1][:], emb[P : 2 * P, :])
+        nc.sync.dma_start(place[1][:], pos[P : 2 * P, :])
 
-        raw, place = [], []
-        for b in range(BLOCKS):
-            rows = slice(b * P, (b + 1) * P)
-            raw.append(held.tile([P, S], F32, name=f"raw{b}"))
-            place.append(held.tile([P, H], F32, name=f"place{b}"))
-            nc.scalar.dma_start(raw[b][:], emb[rows, :])
-            nc.sync.dma_start(place[b][:], pos[rows, :])
-
-        table = [held.tile([P, S], F32, name=f"table{b}") for b in range(BLOCKS)]
-        nc.vector.tensor_scalar_mul(table[0][:], raw[0][:], SCALE)
-        nc.scalar.mul(table[1][:], raw[1][:], SCALE)
+        place_16th = held.tile([P, H], F32, name="place_16th")
+        nc.vector.tensor_scalar_mul(place_16th[:], place[0][:], 1.0 / SCALE)
+        table_16 = held.tile([P, S], F32, name="table_16")
+        nc.scalar.mul(table_16[:], raw[1][:], SCALE)
+        window = [raw[0], table_16]
+        addend = [place_16th, place[1]]
 
         for b in range(BLOCKS):
             rows = slice(b * P, (b + 1) * P)
@@ -36,5 +38,7 @@ def tile_musictransformercontinuoustoken_kernel(tc, emb, pos, offs, out):
             for k in range(K):
                 columns = slice(k * H, (k + 1) * H)
                 tokens = offsets[:, k * LIST_COLUMNS : (k + 1) * LIST_COLUMNS]
-                nc.vector.tensor_tensor(result[:, columns], table[b][:].indirect(tokens), place[b][:], ADD)
+                nc.vector.tensor_tensor(result[:, columns], window[b][:].indirect(tokens), addend[b][:], ADD)
+                if b == 0:
+                    nc.scalar.mul(result[:, columns], result[:, columns], SCALE)
                 nc.sync.dma_start(out[rows, columns], result[:, columns])

@@ -23,7 +23,7 @@ def tile_musictransformercontinuoustoken_kernel(tc, emb, pos, offs, out):
         nc.sync.dma_start(place[0][:], pos[0:P, :])
         nc.sync.dma_start(offsets[:], offs)
         nc.scalar.dma_start(raw[1][:], emb[P : 2 * P, :])
-        nc.sync.dma_start(place[1][:], pos[P : 2 * P, :])
+        nc.scalar.dma_start(place[1][:], pos[P : 2 * P, :])
 
         place_16th = held.tile([P, H], F32, name="place_16th")
         nc.vector.tensor_scalar_mul(place_16th[:], place[0][:], 1.0 / SCALE)

@@ -32,13 +32,19 @@ def tile_musictransformercontinuoustoken_kernel(tc, emb, pos, offs, out):
         window = [raw[0], table_16]
         addend = [place_16th, place[1]]
 
+        TAPER = [H // 2, H // 4, H // 4]
         for b in range(BLOCKS):
             rows = slice(b * P, (b + 1) * P)
             result = held.tile([P, N], F32, name=f"result{b}")
             for k in range(K):
-                columns = slice(k * H, (k + 1) * H)
-                tokens = offsets[:, k * LIST_COLUMNS : (k + 1) * LIST_COLUMNS]
-                nc.vector.tensor_tensor(result[:, columns], window[b][:].indirect(tokens), addend[b][:], ADD)
-                if b == 0:
-                    nc.scalar.mul(result[:, columns], result[:, columns], SCALE)
-                nc.sync.dma_start(out[rows, columns], result[:, columns])
+                last_sequence = b == BLOCKS - 1 and k == K - 1
+                first_place = 0
+                for width in TAPER if last_sequence else [H]:
+                    places = slice(first_place, first_place + width)
+                    columns = slice(k * H + first_place, k * H + first_place + width)
+                    tokens = offsets[:, columns.start // 16 : columns.stop // 16]
+                    nc.vector.tensor_tensor(result[:, columns], window[b][:].indirect(tokens), addend[b][:, places], ADD)
+                    if b == 0:
+                        nc.scalar.mul(result[:, columns], result[:, columns], SCALE)
+                    nc.sync.dma_start(out[rows, columns], result[:, columns])
+                    first_place += width

@@ -32,7 +32,7 @@ def tile_musictransformercontinuoustoken_kernel(tc, emb, pos, offs, out):
         window = [raw[0], table_16]
         addend = [place_16th, place[1]]
 
-        TAPER = [H // 2, H // 4, H // 4]
+        TAPER = [H // 2, H // 2]
         for b in range(BLOCKS):
             rows = slice(b * P, (b + 1) * P)
             result = held.tile([P, N], F32, name=f"result{b}")

@@ -23,7 +23,7 @@ def tile_musictransformercontinuoustoken_kernel(tc, emb, pos, offs, out):
         nc.sync.dma_start(place[0][:], pos[0:P, :])
         nc.sync.dma_start(offsets[:], offs)
         nc.scalar.dma_start(raw[1][:], emb[P : 2 * P, :])
-        nc.scalar.dma_start(place[1][:], pos[P : 2 * P, :])
+        nc.sync.dma_start(place[1][:], pos[P : 2 * P, :])
 
         place_16th = held.tile([P, H], F32, name="place_16th")
         nc.vector.tensor_scalar_mul(place_16th[:], place[0][:], 1.0 / SCALE)

@@ -9,7 +9,6 @@ C, S, K, H = 256, 512, 4, 256
 N = K * H
 SCALE = 16.0
 BLOCKS = C // P
-LIST_COLUMNS = H // 16
 
 
 def tile_musictransformercontinuoustoken_kernel(tc, emb, pos, offs, out):
@@ -25,26 +24,32 @@ def tile_musictransformercontinuoustoken_kernel(tc, emb, pos, offs, out):
         nc.scalar.dma_start(raw[1][:], emb[P : 2 * P, :])
         nc.sync.dma_start(place[1][:], pos[P : 2 * P, :])
 
-        place_16th = held.tile([P, H], F32, name="place_16th")
-        nc.vector.tensor_scalar_mul(place_16th[:], place[0][:], 1.0 / SCALE)
+        place_16th_twice = held.tile([P, 2 * H], F32, name="place_16th_twice")
+        for copy in range(2):
+            nc.vector.tensor_scalar_mul(place_16th_twice[:, copy * H : (copy + 1) * H], place[0][:], 1.0 / SCALE)
         table_16 = held.tile([P, S], F32, name="table_16")
         nc.scalar.mul(table_16[:], raw[1][:], SCALE)
         window = [raw[0], table_16]
-        addend = [place_16th, place[1]]
+        addend = [place_16th_twice, place[1]]
+        result = [held.tile([P, N], F32, name=f"result{b}") for b in range(BLOCKS)]
 
-        TAPER = [H // 2, H // 2]
-        for b in range(BLOCKS):
-            rows = slice(b * P, (b + 1) * P)
-            result = held.tile([P, N], F32, name=f"result{b}")
-            for k in range(K):
-                last_sequence = b == BLOCKS - 1 and k == K - 1
-                first_place = 0
-                for width in TAPER if last_sequence else [H]:
-                    places = slice(first_place, first_place + width)
-                    columns = slice(k * H + first_place, k * H + first_place + width)
-                    tokens = offsets[:, columns.start // 16 : columns.stop // 16]
-                    nc.vector.tensor_tensor(result[:, columns], window[b][:].indirect(tokens), addend[b][:, places], ADD)
-                    if b == 0:
-                        nc.scalar.mul(result[:, columns], result[:, columns], SCALE)
-                    nc.sync.dma_start(out[rows, columns], result[:, columns])
-                    first_place += width
+        def look_up(b, columns):
+            tokens = offsets[:, columns.start // 16 : columns.stop // 16]
+            first_place = columns.start % H
+            places = slice(first_place, first_place + columns.stop - columns.start)
+            nc.vector.tensor_tensor(result[b][:, columns], window[b][:].indirect(tokens), addend[b][:, places], ADD)
+
+        def store(b, columns):
+            nc.sync.dma_start(out[b * P : (b + 1) * P, columns], result[b][:, columns])
+
+        for pair in range(K // 2):
+            look_up(0, slice(pair * 2 * H, (pair + 1) * 2 * H))
+            for k in (2 * pair, 2 * pair + 1):
+                sequence = slice(k * H, (k + 1) * H)
+                nc.scalar.mul(result[0][:, sequence], result[0][:, sequence], SCALE)
+                store(0, sequence)
+
+        bounds = [k * H for k in range(K)] + [N - H // 2, N]
+        for start, stop in zip(bounds, bounds[1:]):
+            look_up(1, slice(start, stop))
+            store(1, slice(start, stop))

import concourse.mybir as mybir

F32 = mybir.dt.float32
U16 = mybir.dt.uint16
ADD = mybir.AluOpType.add

P = 128
C, S, K, H = 256, 512, 4, 256
N = K * H
SCALE = 16.0
BLOCKS = C // P


def tile_musictransformercontinuoustoken_kernel(tc, emb, pos, offs, out):
    nc = tc.nc
    with tc.tile_pool(name="held", bufs=1) as held:
        offsets = held.tile([P, N // 16], U16, name="offsets")
        raw = [held.tile([P, S], F32, name=f"raw{b}") for b in range(BLOCKS)]
        place = [held.tile([P, H], F32, name=f"place{b}") for b in range(BLOCKS)]

        nc.scalar.dma_start(raw[0][:], emb[0:P, :])
        nc.sync.dma_start(place[0][:], pos[0:P, :])
        nc.sync.dma_start(offsets[:], offs)
        nc.scalar.dma_start(raw[1][:], emb[P : 2 * P, :])
        nc.sync.dma_start(place[1][:], pos[P : 2 * P, :])

        place_16th_twice = held.tile([P, 2 * H], F32, name="place_16th_twice")
        for copy in range(2):
            nc.vector.tensor_scalar_mul(place_16th_twice[:, copy * H : (copy + 1) * H], place[0][:], 1.0 / SCALE)
        table_16 = held.tile([P, S], F32, name="table_16")
        nc.scalar.mul(table_16[:], raw[1][:], SCALE)
        window = [raw[0], table_16]
        addend = [place_16th_twice, place[1]]
        result = [held.tile([P, N], F32, name=f"result{b}") for b in range(BLOCKS)]

        def look_up(b, columns):
            tokens = offsets[:, columns.start // 16 : columns.stop // 16]
            first_place = columns.start % H
            places = slice(first_place, first_place + columns.stop - columns.start)
            nc.vector.tensor_tensor(result[b][:, columns], window[b][:].indirect(tokens), addend[b][:, places], ADD)

        def store(b, columns):
            nc.sync.dma_start(out[b * P : (b + 1) * P, columns], result[b][:, columns])

        for pair in range(K // 2):
            look_up(0, slice(pair * 2 * H, (pair + 1) * 2 * H))
            for k in (2 * pair, 2 * pair + 1):
                sequence = slice(k * H, (k + 1) * H)
                nc.scalar.mul(result[0][:, sequence], result[0][:, sequence], SCALE)
                store(0, sequence)

        bounds = [k * H for k in range(K)] + [N - H // 2, N]
        for start, stop in zip(bounds, bounds[1:]):
            look_up(1, slice(start, stop))
            store(1, slice(start, stop))
